import numpy as np
import ml_dtypes


def mxq(x, axis, fmt="e4m3"):
    dtype, down = {"e4m3": (ml_dtypes.float8_e4m3fn, 7), "e5m2": (ml_dtypes.float8_e5m2, 14)}[fmt]
    v = np.moveaxis(np.asarray(x, np.float32).astype(ml_dtypes.bfloat16).astype(np.float64), axis, -1)
    blocks = v.reshape(v.shape[:-1] + (-1, 32))
    amax = np.abs(blocks).max(-1, keepdims=True)
    byte = np.maximum(np.where(amax > 0, np.frexp(amax)[1] - 1 + 127, 0) - down, 1)
    scale = np.exp2(byte - 127.0)
    codes = (blocks / scale).astype(np.float32).astype(dtype).astype(np.float64)
    return np.moveaxis((codes * scale).reshape(v.shape), -1, axis)


WIDE = False


def mx_kscale(k):
    if not WIDE:
        return np.ones(k)
    levels = np.array([10, -10, 5, -5, 0])
    a = np.random.permutation(np.resize(levels, k // 512 * 4)).reshape(k // 512, 4)
    idx = np.arange(k)
    return np.exp2(a[idx // 512, idx % 128 // 32])


BF16 = ml_dtypes.bfloat16


def bf(x):
    return np.asarray(x, np.float32).astype(BF16)


def f64(x):
    return np.asarray(x).astype(np.float64)


N, NS, NV, H, XYZ = 1024, 1024, 512, 8, 3
D = NS // H
COMB = NS + NV
EPS_NORM = 1e-8


def norm_no_nan(x):
    return np.sqrt(np.maximum(np.sum(np.square(x), axis=-1), EPS_NORM))


def setup_inputs():
    c = mx_kscale(COMB)
    cs, cv = c[:NS], c[NS:]
    return {"s": bf(np.random.standard_normal((N, NS)) * cs),
            "v": bf(np.random.standard_normal((N, NV, XYZ)) * 0.6 * cv[:, None]),
            "Wq": bf(np.random.standard_normal((COMB, NS)) * 1.6 / np.sqrt(COMB) / c[:, None]),
            "bq": bf(np.random.standard_normal(NS) * 0.2),
            "Wk": bf(np.random.standard_normal((COMB, NS)) * 1.6 / np.sqrt(COMB) / c[:, None]),
            "bk": bf(np.random.standard_normal(NS) * 0.2)}


def reference(s, v, Wq, bq, Wk, bk):
    v_norm = norm_no_nan(f64(v))
    comb = np.concatenate([f64(s), v_norm], axis=-1)
    cq = mxq(comb, 1, "e4m3")
    q = ((cq @ mxq(f64(Wq), 0, "e4m3")) + f64(bq)).reshape(N, H, D)
    k = ((cq @ mxq(f64(Wk), 0, "e4m3")) + f64(bk)).reshape(N, H, D)
    return q, k

@@ -1,0 +1,219 @@
+import concourse.mybir as mybir
+from concourse.masks import make_identity
+
+F32 = mybir.dt.float32
+BF16 = mybir.dt.bfloat16
+U32 = mybir.dt.uint32
+U8 = mybir.dt.uint8
+FP8X4 = mybir.dt.float8_e4m3fn_x4
+ACT = mybir.ActivationFunctionType
+ALU = mybir.AluOpType
+
+P = 128
+PACK = 4
+K_PASS = P * PACK
+NODES, NS, NV, XYZ = 1024, 1024, 512, 3
+FEATURES = 1024
+S_PASSES = NS // K_PASS
+PASSES = (NS + NV) // K_PASS
+NODE_TILES = NODES // P
+PAIRS = NODE_TILES // 2
+N_TILE = 512
+BANKS = FEATURES // N_TILE
+EARLY_TILES = 4
+NORM_FLOOR = 1e-4
+SQRT_GUARD = 1e-30
+
+FLOPS = 2 * NODES * (NS + NV) * 2 * FEATURES
+
+
+def tile_multiattentivegvplayer_pa_kernel(tc, s, v, Wq, bq, Wk, bk, out_0, out_1):
+    nc = tc.nc
+    weights = (Wq, Wk)
+    biases = (bq, bk)
+    s_rows = s.rearrange("(p t) k -> p t k", t=NODE_TILES)
+    v_rows = v.rearrange("(p t) j c -> p t (j c)", t=NODE_TILES)
+    out_rows = (
+        out_0.rearrange("(p t) h d -> p t (h d)", t=NODE_TILES),
+        out_1.rearrange("(p t) h d -> p t (h d)", t=NODE_TILES),
+    )
+
+    with tc.tile_pool(name="keep", bufs=1) as keep, tc.tile_pool(
+        name="stage", bufs=3
+    ) as stage, tc.tile_pool(name="wide", bufs=4) as wide, tc.psum_pool(
+        name="flip", bufs=2
+    ) as flip, tc.psum_pool(name="acc", bufs=4) as acc_pool:
+        bias_sb = keep.tile([P, 2 * FEATURES], BF16)
+        for proj in range(2):
+            nc.scalar.dma_start(
+                out=bias_sb[:, proj * FEATURES : (proj + 1) * FEATURES],
+                in_=biases[proj].partition_broadcast(P),
+            )
+        ident = keep.tile([P, P], F32)
+        make_identity(nc, ident[:])
+        one = keep.tile([P, 1], F32)
+        nc.vector.memset(one[:], 1.0)
+        root = keep.tile([P, 1], F32)
+        nc.scalar.activation(out=root[:], in_=one[:], func=ACT.Sqrt)
+
+        s_sb = []
+        v_sb = []
+        w_raw = [[], []]
+
+        def load_nodes(pair):
+            tiles = slice(2 * pair, 2 * pair + 2)
+            v_pair = keep.tile([P, 2, NV * XYZ], BF16, name="v_pair%d" % pair)
+            nc.sync.dma_start(out=v_pair[:], in_=v_rows[:, tiles, :])
+            v_sb.append(v_pair)
+            s_pair = keep.tile([P, 2, NS], BF16, name="s_pair%d" % pair)
+            nc.sync.dma_start(out=s_pair[:], in_=s_rows[:, tiles, :])
+            s_sb.append(s_pair)
+
+        def load_weights(proj):
+            w = weights[proj]
+            for g in range(PASSES):
+                raw = keep.tile([P, PACK, FEATURES], BF16, name="w_raw%d_%d" % (proj, g))
+                rows = w[g * K_PASS : (g + 1) * K_PASS, :]
+                if g < S_PASSES:
+                    nc.sync.dma_start(
+                        out=raw[:].rearrange("q (u e) c -> q u e c", u=2),
+                        in_=rows.rearrange("(u q e) c -> q u e c", u=2, e=2),
+                    )
+                else:
+                    nc.sync.dma_start(out=raw[:], in_=rows.rearrange("(t q) c -> q t c", q=P))
+                w_raw[proj].append(raw)
+
+        load_nodes(0)
+        load_weights(0)
+        load_nodes(1)
+        load_weights(1)
+        load_nodes(2)
+        load_nodes(3)
+
+        w_codes = keep.tile([P, PASSES, 2 * FEATURES], U32, align_bytes=64)
+        w_scales = keep.tile([P, PASSES, 2 * FEATURES], U8, align_bytes=64)
+        c_codes = keep.tile([P, NODE_TILES, PASSES * P], U32, align_bytes=64)
+        c_scales = keep.tile([P, NODE_TILES, PASSES * P], U8, align_bytes=64)
+
+        def regroup_weights(proj, g):
+            grouped_halves = []
+            for half in range(BANKS):
+                cols = slice(half * N_TILE, (half + 1) * N_TILE)
+                grouped = wide.tile([P, N_TILE, PACK], BF16, align_bytes=64, name="w_grouped")
+                dst = grouped[:].rearrange("p (c i) t -> p c t i", i=4)
+                src = w_raw[proj][g][:, :, cols].rearrange("p t (c i) -> p c t i", i=4)
+                if half % 2 == 0:
+                    nc.scalar.copy(out=dst, in_=src)
+                else:
+                    nc.vector.tensor_copy(out=dst, in_=src)
+                grouped_halves.append(grouped)
+            return grouped_halves
+
+        def quantise_weights(proj, g, grouped_halves):
+            for half in range(BANKS):
+                first = proj * FEATURES + half * N_TILE
+                cols = slice(first, first + N_TILE)
+                nc.vector.quantize_mx(
+                    out=w_codes[:, g, cols].bitcast(FP8X4),
+                    scales=w_scales[:, g, cols],
+                    in_=grouped_halves[half][:].rearrange("p w t -> p (w t)"),
+                )
+
+        def prepare_weights(proj):
+            waiting = regroup_weights(proj, 0)
+            for g in range(1, PASSES):
+                fresh = regroup_weights(proj, g)
+                quantise_weights(proj, g - 1, waiting)
+                waiting = fresh
+            quantise_weights(proj, PASSES - 1, waiting)
+
+        def prepare_nodes(m):
+            pair, i = m // 2, m % 2
+            sq = stage.tile([P, XYZ, NV], F32)
+            nc.scalar.activation(
+                out=sq[:],
+                in_=v_sb[pair][:, i, :].rearrange("p (j c) -> p c j", c=XYZ),
+                func=ACT.Square,
+            )
+
+            s_words = s_sb[pair][:].bitcast(F32)
+            s_flip = flip.tile([P, 2 * S_PASSES, P], F32)
+            for b in range(2 * S_PASSES):
+                nc.tensor.transpose(s_flip[:, b, :], s_words[:, i, b * P : (b + 1) * P], ident[:])
+            n_flip = flip.tile([P, PACK, P], F32)
+            for t in range(PACK):
+                for c in range(XYZ):
+                    nc.tensor.matmul(
+                        out=n_flip[:, t, :],
+                        lhsT=sq[:, c, t * P : (t + 1) * P],
+                        rhs=ident[:],
+                        is_transpose=True,
+                        start=(c == 0),
+                        stop=(c == XYZ - 1),
+                    )
+
+            s_grouped = stage.tile([P, S_PASSES, P, PACK], BF16, align_bytes=64)
+            nc.scalar.copy(
+                out=s_grouped[:].bitcast(F32),
+                in_=s_flip[:].rearrange("p (g u) r -> p g r u", u=2),
+            )
+            n_root = stage.tile([P, P, PACK], BF16)
+            nc.scalar.activation(
+                out=n_root[:],
+                in_=n_flip[:].rearrange("p t r -> p r t"),
+                func=ACT.Sqrt,
+                bias=SQRT_GUARD,
+            )
+            n_grouped = stage.tile([P, P, PACK], BF16, align_bytes=64)
+            nc.vector.tensor_scalar_max(out=n_grouped[:], in0=n_root[:], scalar1=NORM_FLOOR)
+            nc.vector.quantize_mx(
+                out=c_codes[:, m, 0 : S_PASSES * P].bitcast(FP8X4),
+                scales=c_scales[:, m, 0 : S_PASSES * P],
+                in_=s_grouped[:].rearrange("p g r t -> p (g r t)"),
+            )
+            nc.vector.quantize_mx(
+                out=c_codes[:, m, S_PASSES * P : PASSES * P].bitcast(FP8X4),
+                scales=c_scales[:, m, S_PASSES * P : PASSES * P],
+                in_=n_grouped[:].rearrange("p r t -> p (r t)"),
+            )
+
+        def project(m, proj):
+            result = wide.tile([P, FEATURES], F32)
+            for bank in range(BANKS):
+                first = proj * FEATURES + bank * N_TILE
+                cols = slice(first, first + N_TILE)
+                acc = acc_pool.tile([P, N_TILE], F32)
+                for g in range(PASSES):
+                    rows = slice(g * P, (g + 1) * P)
+                    nc.tensor.matmul_mx(
+                        out=acc[:],
+                        lhsT=c_codes[:, m, rows].bitcast(FP8X4),
+                        lhsT_scale=c_scales[:, m, rows],
+                        rhs=w_codes[:, g, cols].bitcast(FP8X4),
+                        rhs_scale=w_scales[:, g, cols],
+                        start=(g == 0),
+                        stop=(g == PASSES - 1),
+                    )
+                nc.vector.tensor_tensor(
+                    out=result[:, bank * N_TILE : (bank + 1) * N_TILE],
+                    in0=acc[:],
+                    in1=bias_sb[:, cols],
+                    op=ALU.add,
+                )
+            nc.sync.dma_start(out=out_rows[proj][:, m, :], in_=result[:])
+
+        prepare_nodes(0)
+        prepare_nodes(1)
+        prepare_weights(0)
+        project(0, 0)
+        project(1, 0)
+        for m in range(2, EARLY_TILES):
+            prepare_nodes(m)
+            project(m, 0)
+        prepare_weights(1)
+        for m in range(EARLY_TILES):
+            project(m, 1)
+        for m in range(EARLY_TILES, NODE_TILES):
+            prepare_nodes(m)
+            project(m, 0)
+            project(m, 1)

@@ -20,7 +20,7 @@ NODE_TILES = NODES // P
 PAIRS = NODE_TILES // 2
 N_TILE = 512
 BANKS = FEATURES // N_TILE
-EARLY_TILES = 4
+WK_FIRST_ROUND = 2
 NORM_FLOOR = 1e-4
 SQRT_GUARD = 1e-30
 
@@ -39,16 +39,10 @@ def tile_multiattentivegvplayer_pa_kernel(tc, s, v, Wq, bq, Wk, bk, out_0, out_1
     )
 
     with tc.tile_pool(name="keep", bufs=1) as keep, tc.tile_pool(
-        name="stage", bufs=3
+        name="stage", bufs=4
     ) as stage, tc.tile_pool(name="wide", bufs=4) as wide, tc.psum_pool(
         name="flip", bufs=2
     ) as flip, tc.psum_pool(name="acc", bufs=4) as acc_pool:
-        bias_sb = keep.tile([P, 2 * FEATURES], BF16)
-        for proj in range(2):
-            nc.scalar.dma_start(
-                out=bias_sb[:, proj * FEATURES : (proj + 1) * FEATURES],
-                in_=biases[proj].partition_broadcast(P),
-            )
         ident = keep.tile([P, P], F32)
         make_identity(nc, ident[:])
         one = keep.tile([P, 1], F32)
@@ -59,6 +53,7 @@ def tile_multiattentivegvplayer_pa_kernel(tc, s, v, Wq, bq, Wk, bk, out_0, out_1
         s_sb = []
         v_sb = []
         w_raw = [[], []]
+        bias_sb = keep.tile([P, 2 * FEATURES], BF16)
 
         def load_nodes(pair):
             tiles = slice(2 * pair, 2 * pair + 2)
@@ -69,25 +64,31 @@ def tile_multiattentivegvplayer_pa_kernel(tc, s, v, Wq, bq, Wk, bk, out_0, out_1
             nc.sync.dma_start(out=s_pair[:], in_=s_rows[:, tiles, :])
             s_sb.append(s_pair)
 
-        def load_weights(proj):
-            w = weights[proj]
-            for g in range(PASSES):
-                raw = keep.tile([P, PACK, FEATURES], BF16, name="w_raw%d_%d" % (proj, g))
-                rows = w[g * K_PASS : (g + 1) * K_PASS, :]
-                if g < S_PASSES:
-                    nc.sync.dma_start(
-                        out=raw[:].rearrange("q (u e) c -> q u e c", u=2),
-                        in_=rows.rearrange("(u q e) c -> q u e c", u=2, e=2),
-                    )
-                else:
-                    nc.sync.dma_start(out=raw[:], in_=rows.rearrange("(t q) c -> q t c", q=P))
-                w_raw[proj].append(raw)
+        def load_weights(proj, g):
+            raw = keep.tile([P, PACK, FEATURES], BF16, name="w_raw%d_%d" % (proj, g))
+            rows = weights[proj][g * K_PASS : (g + 1) * K_PASS, :]
+            if g < S_PASSES:
+                nc.sync.dma_start(
+                    out=raw[:].rearrange("q (u e) c -> q u e c", u=2),
+                    in_=rows.rearrange("(u q e) c -> q u e c", u=2, e=2),
+                )
+            else:
+                nc.sync.dma_start(out=raw[:], in_=rows.rearrange("(t q) c -> q t c", q=P))
+            w_raw[proj].append(raw)
 
         load_nodes(0)
-        load_weights(0)
+        for g in range(PASSES):
+            load_weights(0, g)
         load_nodes(1)
-        load_weights(1)
+        for proj in range(2):
+            nc.sync.dma_start(
+                out=bias_sb[:, proj * FEATURES : (proj + 1) * FEATURES],
+                in_=biases[proj].partition_broadcast(P),
+            )
+        load_weights(1, 0)
         load_nodes(2)
+        load_weights(1, 1)
+        load_weights(1, 2)
         load_nodes(3)
 
         w_codes = keep.tile([P, PASSES, 2 * FEATURES], U32, align_bytes=64)
@@ -95,39 +96,30 @@ def tile_multiattentivegvplayer_pa_kernel(tc, s, v, Wq, bq, Wk, bk, out_0, out_1
         c_codes = keep.tile([P, NODE_TILES, PASSES * P], U32, align_bytes=64)
         c_scales = keep.tile([P, NODE_TILES, PASSES * P], U8, align_bytes=64)
 
-        def regroup_weights(proj, g):
-            grouped_halves = []
-            for half in range(BANKS):
-                cols = slice(half * N_TILE, (half + 1) * N_TILE)
-                grouped = wide.tile([P, N_TILE, PACK], BF16, align_bytes=64, name="w_grouped")
-                dst = grouped[:].rearrange("p (c i) t -> p c t i", i=4)
-                src = w_raw[proj][g][:, :, cols].rearrange("p t (c i) -> p c t i", i=4)
-                if half % 2 == 0:
-                    nc.scalar.copy(out=dst, in_=src)
-                else:
-                    nc.vector.tensor_copy(out=dst, in_=src)
-                grouped_halves.append(grouped)
-            return grouped_halves
+        def regroup_weights(proj, g, bank, on_scalar):
+            cols = slice(bank * N_TILE, (bank + 1) * N_TILE)
+            grouped = wide.tile([P, N_TILE, PACK], BF16, align_bytes=64, name="w_grouped")
+            dst = grouped[:].rearrange("p (c i) t -> p c t i", i=4)
+            src = w_raw[proj][g][:, :, cols].rearrange("p t (c i) -> p c t i", i=4)
+            if on_scalar:
+                nc.scalar.copy(out=dst, in_=src)
+            else:
+                nc.vector.tensor_copy(out=dst, in_=src)
+            return grouped
 
-        def quantise_weights(proj, g, grouped_halves):
-            for half in range(BANKS):
-                first = proj * FEATURES + half * N_TILE
-                cols = slice(first, first + N_TILE)
-                nc.vector.quantize_mx(
-                    out=w_codes[:, g, cols].bitcast(FP8X4),
-                    scales=w_scales[:, g, cols],
-                    in_=grouped_halves[half][:].rearrange("p w t -> p (w t)"),
-                )
+        def quantise_weights(proj, g, bank, grouped):
+            first = proj * FEATURES + bank * N_TILE
+            cols = slice(first, first + N_TILE)
+            nc.vector.quantize_mx(
+                out=w_codes[:, g, cols].bitcast(FP8X4),
+                scales=w_scales[:, g, cols],
+                in_=grouped[:].rearrange("p w t -> p (w t)"),
+            )
 
-        def prepare_weights(proj):
-            waiting = regroup_weights(proj, 0)
-            for g in range(1, PASSES):
-                fresh = regroup_weights(proj, g)
-                quantise_weights(proj, g - 1, waiting)
-                waiting = fresh
-            quantise_weights(proj, PASSES - 1, waiting)
+        squares = {}
+        grouped_nodes = {}
 
-        def prepare_nodes(m):
+        def square(m):
             pair, i = m // 2, m % 2
             sq = stage.tile([P, XYZ, NV], F32)
             nc.scalar.activation(
@@ -135,7 +127,11 @@ def tile_multiattentivegvplayer_pa_kernel(tc, s, v, Wq, bq, Wk, bk, out_0, out_1
                 in_=v_sb[pair][:, i, :].rearrange("p (j c) -> p c j", c=XYZ),
                 func=ACT.Square,
             )
+            squares[m] = sq
 
+        def flip_nodes(m):
+            pair, i = m // 2, m % 2
+            sq = squares[m]
             s_words = s_sb[pair][:].bitcast(F32)
             s_flip = flip.tile([P, 2 * S_PASSES, P], F32)
             for b in range(2 * S_PASSES):
@@ -151,7 +147,6 @@ def tile_multiattentivegvplayer_pa_kernel(tc, s, v, Wq, bq, Wk, bk, out_0, out_1
                         start=(c == 0),
                         stop=(c == XYZ - 1),
                     )
-
             s_grouped = stage.tile([P, S_PASSES, P, PACK], BF16, align_bytes=64)
             nc.scalar.copy(
                 out=s_grouped[:].bitcast(F32),
@@ -164,6 +159,10 @@ def tile_multiattentivegvplayer_pa_kernel(tc, s, v, Wq, bq, Wk, bk, out_0, out_1
                 func=ACT.Sqrt,
                 bias=SQRT_GUARD,
             )
+            grouped_nodes[m] = (s_grouped, n_root)
+
+        def quantise_nodes(m):
+            s_grouped, n_root = grouped_nodes[m]
             n_grouped = stage.tile([P, P, PACK], BF16, align_bytes=64)
             nc.vector.tensor_scalar_max(out=n_grouped[:], in0=n_root[:], scalar1=NORM_FLOOR)
             nc.vector.quantize_mx(
@@ -177,43 +176,67 @@ def tile_multiattentivegvplayer_pa_kernel(tc, s, v, Wq, bq, Wk, bk, out_0, out_1
                 in_=n_grouped[:].rearrange("p r t -> p (r t)"),
             )
 
-        def project(m, proj):
-            result = wide.tile([P, FEATURES], F32)
-            for bank in range(BANKS):
-                first = proj * FEATURES + bank * N_TILE
-                cols = slice(first, first + N_TILE)
-                acc = acc_pool.tile([P, N_TILE], F32)
-                for g in range(PASSES):
-                    rows = slice(g * P, (g + 1) * P)
-                    nc.tensor.matmul_mx(
-                        out=acc[:],
-                        lhsT=c_codes[:, m, rows].bitcast(FP8X4),
-                        lhsT_scale=c_scales[:, m, rows],
-                        rhs=w_codes[:, g, cols].bitcast(FP8X4),
-                        rhs_scale=w_scales[:, g, cols],
-                        start=(g == 0),
-                        stop=(g == PASSES - 1),
-                    )
-                nc.vector.tensor_tensor(
-                    out=result[:, bank * N_TILE : (bank + 1) * N_TILE],
-                    in0=acc[:],
-                    in1=bias_sb[:, cols],
-                    op=ALU.add,
+        def project_bank(m, proj, bank, result):
+            first = proj * FEATURES + bank * N_TILE
+            cols = slice(first, first + N_TILE)
+            acc = acc_pool.tile([P, N_TILE], F32)
+            for g in range(PASSES):
+                rows = slice(g * P, (g + 1) * P)
+                nc.tensor.matmul_mx(
+                    out=acc[:],
+                    lhsT=c_codes[:, m, rows].bitcast(FP8X4),
+                    lhsT_scale=c_scales[:, m, rows],
+                    rhs=w_codes[:, g, cols].bitcast(FP8X4),
+                    rhs_scale=w_scales[:, g, cols],
+                    start=(g == 0),
+                    stop=(g == PASSES - 1),
                 )
+            nc.vector.tensor_tensor(
+                out=result[:, bank * N_TILE : (bank + 1) * N_TILE],
+                in0=acc[:],
+                in1=bias_sb[:, cols],
+                op=ALU.add,
+            )
+
+        def store(m, proj, result):
             nc.sync.dma_start(out=out_rows[proj][:, m, :], in_=result[:])
 
-        prepare_nodes(0)
-        prepare_nodes(1)
-        prepare_weights(0)
-        project(0, 0)
-        project(1, 0)
-        for m in range(2, EARLY_TILES):
-            prepare_nodes(m)
-            project(m, 0)
-        prepare_weights(1)
-        for m in range(EARLY_TILES):
-            project(m, 1)
-        for m in range(EARLY_TILES, NODE_TILES):
-            prepare_nodes(m)
-            project(m, 0)
-            project(m, 1)
+        with tc.manual_schedule():
+            square(0)
+            square(1)
+            flip_nodes(0)
+            quantise_nodes(0)
+            waiting = None
+            for g in range(PASSES):
+                fresh = [regroup_weights(0, g, bank, bank == 0) for bank in range(BANKS)]
+                if waiting is not None:
+                    for bank in range(BANKS):
+                        quantise_weights(0, g - 1, bank, waiting[bank])
+                waiting = fresh
+            for bank in range(BANKS):
+                quantise_weights(0, PASSES - 1, bank, waiting[bank])
+
+            for m in range(NODE_TILES):
+                if m + 2 < NODE_TILES:
+                    square(m + 2)
+                if m + 1 < NODE_TILES:
+                    flip_nodes(m + 1)
+                piece = m - WK_FIRST_ROUND
+                result = wide.tile([P, FEATURES], F32, name="result")
+                project_bank(m, 0, 0, result)
+                if piece >= 0:
+                    grouped = regroup_weights(
+                        1, piece % PASSES, piece // PASSES, m + 2 >= NODE_TILES
+                    )
+                if m + 1 < NODE_TILES:
+                    quantise_nodes(m + 1)
+                project_bank(m, 0, 1, result)
+                store(m, 0, result)
+                if piece >= 0:
+                    quantise_weights(1, piece % PASSES, piece // PASSES, grouped)
+
+            for m in range(NODE_TILES):
+                result = wide.tile([P, FEATURES], F32, name="result")
+                for bank in range(BANKS):
+                    project_bank(m, 1, bank, result)
+                store(m, 1, result)

@@ -20,7 +20,7 @@ NODE_TILES = NODES // P
 PAIRS = NODE_TILES // 2
 N_TILE = 512
 BANKS = FEATURES // N_TILE
-WK_FIRST_ROUND = 2
+LAG = 3
 NORM_FLOOR = 1e-4
 SQRT_GUARD = 1e-30
 
@@ -39,7 +39,7 @@ def tile_multiattentivegvplayer_pa_kernel(tc, s, v, Wq, bq, Wk, bk, out_0, out_1
     )
 
     with tc.tile_pool(name="keep", bufs=1) as keep, tc.tile_pool(
-        name="stage", bufs=4
+        name="stage", bufs=3
     ) as stage, tc.tile_pool(name="wide", bufs=4) as wide, tc.psum_pool(
         name="flip", bufs=2
     ) as flip, tc.psum_pool(name="acc", bufs=4) as acc_pool:
@@ -77,19 +77,19 @@ def tile_multiattentivegvplayer_pa_kernel(tc, s, v, Wq, bq, Wk, bk, out_0, out_1
             w_raw[proj].append(raw)
 
         load_nodes(0)
-        for g in range(PASSES):
-            load_weights(0, g)
+        load_weights(0, 0)
+        load_weights(0, 1)
         load_nodes(1)
+        load_weights(0, 2)
         for proj in range(2):
             nc.sync.dma_start(
                 out=bias_sb[:, proj * FEATURES : (proj + 1) * FEATURES],
                 in_=biases[proj].partition_broadcast(P),
             )
-        load_weights(1, 0)
         load_nodes(2)
-        load_weights(1, 1)
-        load_weights(1, 2)
         load_nodes(3)
+        for g in range(PASSES):
+            load_weights(1, g)
 
         w_codes = keep.tile([P, PASSES, 2 * FEATURES], U32, align_bytes=64)
         w_scales = keep.tile([P, PASSES, 2 * FEATURES], U8, align_bytes=64)
@@ -198,45 +198,33 @@ def tile_multiattentivegvplayer_pa_kernel(tc, s, v, Wq, bq, Wk, bk, out_0, out_1
                 op=ALU.add,
             )
 
-        def store(m, proj, result):
+        def project(m, proj):
+            result = wide.tile([P, FEATURES], F32)
+            for bank in range(BANKS):
+                project_bank(m, proj, bank, result)
             nc.sync.dma_start(out=out_rows[proj][:, m, :], in_=result[:])
 
         with tc.manual_schedule():
             square(0)
-            square(1)
-            flip_nodes(0)
-            quantise_nodes(0)
-            waiting = None
-            for g in range(PASSES):
-                fresh = [regroup_weights(0, g, bank, bank == 0) for bank in range(BANKS)]
-                if waiting is not None:
+            for r in range(NODE_TILES):
+                if r + 1 < NODE_TILES:
+                    square(r + 1)
+                flip_nodes(r)
+                if r < PASSES:
+                    fresh = [regroup_weights(0, r, bank, False) for bank in range(BANKS)]
                     for bank in range(BANKS):
-                        quantise_weights(0, g - 1, bank, waiting[bank])
-                waiting = fresh
-            for bank in range(BANKS):
-                quantise_weights(0, PASSES - 1, bank, waiting[bank])
-
+                        quantise_weights(0, r, bank, fresh[bank])
+                quantise_nodes(r)
+                if r >= LAG:
+                    g = r - LAG
+                    if g < PASSES:
+                        grouped = regroup_weights(1, g, 0, False)
+                    project(r - LAG, 0)
+                    if g < PASSES:
+                        quantise_weights(1, g, 0, grouped)
+            late = [regroup_weights(1, g, 1, True) for g in range(PASSES)]
+            for g in range(PASSES):
+                project(NODE_TILES - LAG + g, 0)
+                quantise_weights(1, g, 1, late[g])
             for m in range(NODE_TILES):
-                if m + 2 < NODE_TILES:
-                    square(m + 2)
-                if m + 1 < NODE_TILES:
-                    flip_nodes(m + 1)
-                piece = m - WK_FIRST_ROUND
-                result = wide.tile([P, FEATURES], F32, name="result")
-                project_bank(m, 0, 0, result)
-                if piece >= 0:
-                    grouped = regroup_weights(
-                        1, piece % PASSES, piece // PASSES, m + 2 >= NODE_TILES
-                    )
-                if m + 1 < NODE_TILES:
-                    quantise_nodes(m + 1)
-                project_bank(m, 0, 1, result)
-                store(m, 0, result)
-                if piece >= 0:
-                    quantise_weights(1, piece % PASSES, piece // PASSES, grouped)
-
-            for m in range(NODE_TILES):
-                result = wide.tile([P, FEATURES], F32, name="result")
-                for bank in range(BANKS):
-                    project_bank(m, 1, bank, result)
-                store(m, 1, result)
+                project(m, 1)

@@ -5,6 +5,7 @@ F32 = mybir.dt.float32
 BF16 = mybir.dt.bfloat16
 U32 = mybir.dt.uint32
 U8 = mybir.dt.uint8
+I32 = mybir.dt.int32
 FP8X4 = mybir.dt.float8_e4m3fn_x4
 ACT = mybir.ActivationFunctionType
 ALU = mybir.AluOpType
@@ -50,10 +51,19 @@ def tile_multiattentivegvplayer_pa_kernel(tc, s, v, Wq, bq, Wk, bk, out_0, out_1
         root = keep.tile([P, 1], F32)
         nc.scalar.activation(out=root[:], in_=one[:], func=ACT.Sqrt)
 
+        bias_rows = keep.tile([P, 2 * FEATURES], BF16)
+        nc.vector.memset(bias_rows[:].bitcast(I32), 0)
+        for proj in range(2):
+            nc.scalar.dma_start(
+                out=bias_rows[0:1, proj * FEATURES : (proj + 1) * FEATURES],
+                in_=biases[proj].unsqueeze(0),
+            )
+        ones = keep.tile([P, P], BF16)
+        nc.vector.memset(ones[:], 1.0)
+
         s_sb = []
         v_sb = []
         w_raw = [[], []]
-        bias_sb = keep.tile([P, 2 * FEATURES], BF16)
 
         def load_nodes(pair):
             tiles = slice(2 * pair, 2 * pair + 2)
@@ -81,11 +91,6 @@ def tile_multiattentivegvplayer_pa_kernel(tc, s, v, Wq, bq, Wk, bk, out_0, out_1
         load_weights(0, 1)
         load_nodes(1)
         load_weights(0, 2)
-        for proj in range(2):
-            nc.sync.dma_start(
-                out=bias_sb[:, proj * FEATURES : (proj + 1) * FEATURES],
-                in_=biases[proj].partition_broadcast(P),
-            )
         load_nodes(2)
         load_nodes(3)
         for g in range(PASSES):
@@ -205,6 +210,15 @@ def tile_multiattentivegvplayer_pa_kernel(tc, s, v, Wq, bq, Wk, bk, out_0, out_1
             nc.sync.dma_start(out=out_rows[proj][:, m, :], in_=result[:])
 
         with tc.manual_schedule():
+            bias_sb = keep.tile([P, 2 * FEATURES], F32)
+            for c in range(2 * BANKS):
+                cols = slice(c * N_TILE, (c + 1) * N_TILE)
+                spread = acc_pool.tile([P, N_TILE], F32, name="acc")
+                nc.tensor.matmul(
+                    out=spread[:], lhsT=ones[:], rhs=bias_rows[:, cols], start=True, stop=True
+                )
+                nc.vector.tensor_copy(out=bias_sb[:, cols], in_=spread[:])
+
             square(0)
             for r in range(NODE_TILES):
                 if r + 1 < NODE_TILES:

@@ -92,9 +92,10 @@ def tile_multiattentivegvplayer_pa_kernel(tc, s, v, Wq, bq, Wk, bk, out_0, out_1
         load_nodes(1)
         load_weights(0, 2)
         load_nodes(2)
+        load_weights(1, 0)
+        load_weights(1, 1)
         load_nodes(3)
-        for g in range(PASSES):
-            load_weights(1, g)
+        load_weights(1, 2)
 
         w_codes = keep.tile([P, PASSES, 2 * FEATURES], U32, align_bytes=64)
         w_scales = keep.tile([P, PASSES, 2 * FEATURES], U8, align_bytes=64)
@@ -209,21 +210,25 @@ def tile_multiattentivegvplayer_pa_kernel(tc, s, v, Wq, bq, Wk, bk, out_0, out_1
                 project_bank(m, proj, bank, result)
             nc.sync.dma_start(out=out_rows[proj][:, m, :], in_=result[:])
 
-        with tc.manual_schedule():
-            bias_sb = keep.tile([P, 2 * FEATURES], F32)
+        bias_sb = keep.tile([P, 2 * FEATURES], F32)
+
+        def spread_biases():
             for c in range(2 * BANKS):
                 cols = slice(c * N_TILE, (c + 1) * N_TILE)
                 spread = acc_pool.tile([P, N_TILE], F32, name="acc")
                 nc.tensor.matmul(
                     out=spread[:], lhsT=ones[:], rhs=bias_rows[:, cols], start=True, stop=True
                 )
-                nc.vector.tensor_copy(out=bias_sb[:, cols], in_=spread[:])
+                nc.scalar.copy(out=bias_sb[:, cols], in_=spread[:])
 
+        with tc.manual_schedule():
             square(0)
             for r in range(NODE_TILES):
                 if r + 1 < NODE_TILES:
                     square(r + 1)
                 flip_nodes(r)
+                if r == 0:
+                    spread_biases()
                 if r < PASSES:
                     fresh = [regroup_weights(0, r, bank, False) for bank in range(BANKS)]
                     for bank in range(BANKS):

@@ -198,7 +198,7 @@ def tile_multiattentivegvplayer_pa_kernel(tc, s, v, Wq, bq, Wk, bk, out_0, out_1
                     stop=(g == PASSES - 1),
                 )
             nc.vector.tensor_tensor(
-                out=result[:, bank * N_TILE : (bank + 1) * N_TILE],
+                out=result,
                 in0=acc[:],
                 in1=bias_sb[:, cols],
                 op=ALU.add,
@@ -207,7 +207,7 @@ def tile_multiattentivegvplayer_pa_kernel(tc, s, v, Wq, bq, Wk, bk, out_0, out_1
         def project(m, proj):
             result = wide.tile([P, FEATURES], F32)
             for bank in range(BANKS):
-                project_bank(m, proj, bank, result)
+                project_bank(m, proj, bank, result[:, bank * N_TILE : (bank + 1) * N_TILE])
             nc.sync.dma_start(out=out_rows[proj][:, m, :], in_=result[:])
 
         bias_sb = keep.tile([P, 2 * FEATURES], F32)
@@ -245,5 +245,9 @@ def tile_multiattentivegvplayer_pa_kernel(tc, s, v, Wq, bq, Wk, bk, out_0, out_1
             for g in range(PASSES):
                 project(NODE_TILES - LAG + g, 0)
                 quantise_weights(1, g, 1, late[g])
-            for m in range(NODE_TILES):
-                project(m, 1)
+            for bank in range(BANKS):
+                cols = slice(bank * N_TILE, (bank + 1) * N_TILE)
+                for m in range(NODE_TILES):
+                    half = wide.tile([P, N_TILE], F32)
+                    project_bank(m, 1, bank, half[:])
+                    nc.sync.dma_start(out=out_rows[1][:, m, cols], in_=half[:])

@@ -41,15 +41,19 @@ def tile_multiattentivegvplayer_pa_kernel(tc, s, v, Wq, bq, Wk, bk, out_0, out_1
 
     with tc.tile_pool(name="keep", bufs=1) as keep, tc.tile_pool(
         name="stage", bufs=3
-    ) as stage, tc.tile_pool(name="wide", bufs=4) as wide, tc.psum_pool(
-        name="flip", bufs=2
-    ) as flip, tc.psum_pool(name="acc", bufs=4) as acc_pool:
+    ) as stage, tc.tile_pool(name="wide", bufs=4) as wide, tc.tile_pool(
+        name="q_results", bufs=4
+    ) as q_pool, tc.tile_pool(name="k_results", bufs=8) as k_pool, tc.psum_pool(name="flip", bufs=2) as flip, tc.psum_pool(
+        name="acc", bufs=4
+    ) as acc_pool:
         ident = keep.tile([P, P], F32)
         make_identity(nc, ident[:])
+        ones = keep.tile([P, P], BF16)
+        nc.vector.memset(ones[:], 1.0)
+        filler = keep.tile([P, N_TILE], BF16)
+        nc.vector.memset(filler[:].bitcast(I32), 0)
         one = keep.tile([P, 1], F32)
         nc.vector.memset(one[:], 1.0)
-        root = keep.tile([P, 1], F32)
-        nc.scalar.activation(out=root[:], in_=one[:], func=ACT.Sqrt)
 
         bias_rows = keep.tile([P, 2 * FEATURES], BF16)
         nc.vector.memset(bias_rows[:].bitcast(I32), 0)
@@ -58,23 +62,40 @@ def tile_multiattentivegvplayer_pa_kernel(tc, s, v, Wq, bq, Wk, bk, out_0, out_1
                 out=bias_rows[0:1, proj * FEATURES : (proj + 1) * FEATURES],
                 in_=biases[proj].unsqueeze(0),
             )
-        ones = keep.tile([P, P], BF16)
-        nc.vector.memset(ones[:], 1.0)
+        root = keep.tile([P, 1], F32)
+        nc.scalar.activation(out=root[:], in_=one[:], func=ACT.Sqrt)
 
-        s_sb = []
-        v_sb = []
-        w_raw = [[], []]
+        s_sb = {}
+        v_sb = {}
+        w_raw = {}
 
-        def load_nodes(pair):
-            tiles = slice(2 * pair, 2 * pair + 2)
-            v_pair = keep.tile([P, 2, NV * XYZ], BF16, name="v_pair%d" % pair)
-            nc.sync.dma_start(out=v_pair[:], in_=v_rows[:, tiles, :])
-            v_sb.append(v_pair)
-            s_pair = keep.tile([P, 2, NS], BF16, name="s_pair%d" % pair)
-            nc.sync.dma_start(out=s_pair[:], in_=s_rows[:, tiles, :])
-            s_sb.append(s_pair)
+        def load_v(first, count):
+            v_tiles = keep.tile([P, count, NV * XYZ], BF16, name="v_tiles%d" % first)
+            nc.sync.dma_start(out=v_tiles[:], in_=v_rows[:, first : first + count, :])
+            for i in range(count):
+                v_sb[first + i] = v_tiles[:, i, :]
 
-        def load_weights(proj, g):
+        def load_s(first, count):
+            s_tiles = keep.tile([P, count, NS], BF16, name="s_tiles%d" % first)
+            nc.sync.dma_start(out=s_tiles[:], in_=s_rows[:, first : first + count, :])
+            for i in range(count):
+                s_sb[first + i] = s_tiles[:, i, :]
+
+        def load_columns(proj, g, bank):
+            raw = keep.tile([P, PACK, N_TILE], BF16, name="w_raw%d_%d_%d" % (proj, g, bank))
+            cols = slice(bank * N_TILE, (bank + 1) * N_TILE)
+            rows = weights[proj][g * K_PASS : (g + 1) * K_PASS, cols]
+            if g < S_PASSES:
+                for u in range(2):
+                    nc.sync.dma_start(
+                        out=raw[:, 2 * u : 2 * u + 2, :],
+                        in_=rows[u * 2 * P : (u + 1) * 2 * P, :].rearrange("(q e) c -> q e c", e=2),
+                    )
+            else:
+                nc.sync.dma_start(out=raw[:], in_=rows.rearrange("(t q) c -> q t c", q=P))
+            w_raw[proj, g, bank] = raw[:]
+
+        def load_rows(proj, g):
             raw = keep.tile([P, PACK, FEATURES], BF16, name="w_raw%d_%d" % (proj, g))
             rows = weights[proj][g * K_PASS : (g + 1) * K_PASS, :]
             if g < S_PASSES:
@@ -84,36 +105,43 @@ def tile_multiattentivegvplayer_pa_kernel(tc, s, v, Wq, bq, Wk, bk, out_0, out_1
                 )
             else:
                 nc.sync.dma_start(out=raw[:], in_=rows.rearrange("(t q) c -> q t c", q=P))
-            w_raw[proj].append(raw)
+            for bank in range(BANKS):
+                w_raw[proj, g, bank] = raw[:, :, bank * N_TILE : (bank + 1) * N_TILE]
 
-        load_nodes(0)
-        load_weights(0, 0)
-        load_weights(0, 1)
-        load_nodes(1)
-        load_weights(0, 2)
-        load_nodes(2)
-        load_weights(1, 0)
-        load_weights(1, 1)
-        load_nodes(3)
-        load_weights(1, 2)
+        load_v(0, 2)
+        load_rows(0, 0)
+        load_s(0, 2)
+        load_rows(0, 1)
+        load_v(2, 2)
+        load_s(2, 2)
+        load_rows(0, 2)
+        load_v(4, 2)
+        load_s(4, 2)
+        load_rows(1, 0)
+        load_rows(1, 1)
+        load_v(6, 2)
+        load_s(6, 2)
+        load_rows(1, 2)
 
         w_codes = keep.tile([P, PASSES, 2 * FEATURES], U32, align_bytes=64)
         w_scales = keep.tile([P, PASSES, 2 * FEATURES], U8, align_bytes=64)
         c_codes = keep.tile([P, NODE_TILES, PASSES * P], U32, align_bytes=64)
         c_scales = keep.tile([P, NODE_TILES, PASSES * P], U8, align_bytes=64)
 
-        def regroup_weights(proj, g, bank, on_scalar):
-            cols = slice(bank * N_TILE, (bank + 1) * N_TILE)
+        grouped_weights = {}
+
+        def regroup_weights(proj, g, bank, on_scalar=False):
             grouped = wide.tile([P, N_TILE, PACK], BF16, align_bytes=64, name="w_grouped")
             dst = grouped[:].rearrange("p (c i) t -> p c t i", i=4)
-            src = w_raw[proj][g][:, :, cols].rearrange("p t (c i) -> p c t i", i=4)
+            src = w_raw[proj, g, bank].rearrange("p t (c i) -> p c t i", i=4)
             if on_scalar:
                 nc.scalar.copy(out=dst, in_=src)
             else:
                 nc.vector.tensor_copy(out=dst, in_=src)
-            return grouped
+            grouped_weights[proj, g, bank] = grouped
 
-        def quantise_weights(proj, g, bank, grouped):
+        def quantise_weights(proj, g, bank):
+            grouped = grouped_weights[proj, g, bank]
             first = proj * FEATURES + bank * N_TILE
             cols = slice(first, first + N_TILE)
             nc.vector.quantize_mx(
@@ -123,58 +151,70 @@ def tile_multiattentivegvplayer_pa_kernel(tc, s, v, Wq, bq, Wk, bk, out_0, out_1
             )
 
         squares = {}
-        grouped_nodes = {}
+        grouped_s = {}
+        roots = {}
+        flipped = {}
 
         def square(m):
-            pair, i = m // 2, m % 2
             sq = stage.tile([P, XYZ, NV], F32)
             nc.scalar.activation(
-                out=sq[:],
-                in_=v_sb[pair][:, i, :].rearrange("p (j c) -> p c j", c=XYZ),
-                func=ACT.Square,
+                out=sq[:], in_=v_sb[m].rearrange("p (j c) -> p c j", c=XYZ), func=ACT.Square
             )
             squares[m] = sq
 
-        def flip_nodes(m):
-            pair, i = m // 2, m % 2
-            sq = squares[m]
-            s_words = s_sb[pair][:].bitcast(F32)
-            s_flip = flip.tile([P, 2 * S_PASSES, P], F32)
+        def flip_s(m):
+            s_words = s_sb[m].bitcast(F32)
+            s_flip = flip.tile([P, 2 * S_PASSES, P], F32, name="s_flip")
             for b in range(2 * S_PASSES):
-                nc.tensor.transpose(s_flip[:, b, :], s_words[:, i, b * P : (b + 1) * P], ident[:])
-            n_flip = flip.tile([P, PACK, P], F32)
-            for t in range(PACK):
+                nc.tensor.transpose(s_flip[:, b, :], s_words[:, b * P : (b + 1) * P], ident[:])
+            flipped[m, 0] = s_flip
+
+        def flip_v(m, words=range(PACK)):
+            if words[0] == 0:
+                flipped[m, 1] = flip.tile([P, PACK, P], F32, name="n_flip")
+            for t in words:
                 for c in range(XYZ):
                     nc.tensor.matmul(
-                        out=n_flip[:, t, :],
-                        lhsT=sq[:, c, t * P : (t + 1) * P],
+                        out=flipped[m, 1][:, t, :],
+                        lhsT=squares[m][:, c, t * P : (t + 1) * P],
                         rhs=ident[:],
                         is_transpose=True,
                         start=(c == 0),
                         stop=(c == XYZ - 1),
                     )
+
+        def keep_warm(count):
+            spare = acc_pool.tile([P, N_TILE], F32, name="acc")
+            for i in range(count):
+                nc.tensor.matmul(
+                    out=spare[:], lhsT=ones[:], rhs=filler[:], start=True, stop=True
+                )
+
+        def empty_s(m):
             s_grouped = stage.tile([P, S_PASSES, P, PACK], BF16, align_bytes=64)
             nc.scalar.copy(
                 out=s_grouped[:].bitcast(F32),
-                in_=s_flip[:].rearrange("p (g u) r -> p g r u", u=2),
+                in_=flipped[m, 0][:].rearrange("p (g u) r -> p g r u", u=2),
             )
+            grouped_s[m] = s_grouped
+
+        def empty_v(m):
             n_root = stage.tile([P, P, PACK], BF16)
             nc.scalar.activation(
                 out=n_root[:],
-                in_=n_flip[:].rearrange("p t r -> p r t"),
+                in_=flipped[m, 1][:].rearrange("p t r -> p r t"),
                 func=ACT.Sqrt,
                 bias=SQRT_GUARD,
             )
-            grouped_nodes[m] = (s_grouped, n_root)
+            roots[m] = n_root
 
         def quantise_nodes(m):
-            s_grouped, n_root = grouped_nodes[m]
             n_grouped = stage.tile([P, P, PACK], BF16, align_bytes=64)
-            nc.vector.tensor_scalar_max(out=n_grouped[:], in0=n_root[:], scalar1=NORM_FLOOR)
+            nc.vector.tensor_scalar_max(out=n_grouped[:], in0=roots[m][:], scalar1=NORM_FLOOR)
             nc.vector.quantize_mx(
                 out=c_codes[:, m, 0 : S_PASSES * P].bitcast(FP8X4),
                 scales=c_scales[:, m, 0 : S_PASSES * P],
-                in_=s_grouped[:].rearrange("p g r t -> p (g r t)"),
+                in_=grouped_s[m][:].rearrange("p g r t -> p (g r t)"),
             )
             nc.vector.quantize_mx(
                 out=c_codes[:, m, S_PASSES * P : PASSES * P].bitcast(FP8X4),
@@ -182,14 +222,16 @@ def tile_multiattentivegvplayer_pa_kernel(tc, s, v, Wq, bq, Wk, bk, out_0, out_1
                 in_=n_grouped[:].rearrange("p r t -> p (r t)"),
             )
 
-        def project_bank(m, proj, bank, result):
-            first = proj * FEATURES + bank * N_TILE
-            cols = slice(first, first + N_TILE)
-            acc = acc_pool.tile([P, N_TILE], F32)
-            for g in range(PASSES):
+        sums = {}
+
+        def multiply_columns(m, proj, first, width, passes=range(PASSES)):
+            cols = slice(proj * FEATURES + first, proj * FEATURES + first + width)
+            if passes[0] == 0:
+                sums[m, proj, first] = acc_pool.tile([P, width], F32, name="acc")
+            for g in passes:
                 rows = slice(g * P, (g + 1) * P)
                 nc.tensor.matmul_mx(
-                    out=acc[:],
+                    out=sums[m, proj, first][:],
                     lhsT=c_codes[:, m, rows].bitcast(FP8X4),
                     lhsT_scale=c_scales[:, m, rows],
                     rhs=w_codes[:, g, cols].bitcast(FP8X4),
@@ -197,57 +239,100 @@ def tile_multiattentivegvplayer_pa_kernel(tc, s, v, Wq, bq, Wk, bk, out_0, out_1
                     start=(g == 0),
                     stop=(g == PASSES - 1),
                 )
+
+        q_results = {}
+
+        def finish_columns(m, proj, first, width):
+            if proj == 1:
+                result = k_pool.tile([P, width], F32, name="k_result")[:]
+            else:
+                if first == 0:
+                    q_results[m] = q_pool.tile([P, FEATURES], F32, name="q_result")
+                result = q_results[m][:, first : first + width]
             nc.vector.tensor_tensor(
                 out=result,
-                in0=acc[:],
-                in1=bias_sb[:, cols],
+                in0=sums[m, proj, first][:],
+                in1=bias_sb[:, proj * FEATURES + first : proj * FEATURES + first + width],
                 op=ALU.add,
             )
+            if proj == 1:
+                nc.sync.dma_start(out=out_rows[1][:, m, first : first + width], in_=result)
+            elif first + width == FEATURES:
+                nc.sync.dma_start(out=out_rows[0][:, m, :], in_=q_results[m][:])
 
-        def project(m, proj):
-            result = wide.tile([P, FEATURES], F32)
-            for bank in range(BANKS):
-                project_bank(m, proj, bank, result[:, bank * N_TILE : (bank + 1) * N_TILE])
-            nc.sync.dma_start(out=out_rows[proj][:, m, :], in_=result[:])
+        def multiply(m, proj, bank):
+            multiply_columns(m, proj, bank * N_TILE, N_TILE)
 
-        bias_sb = keep.tile([P, 2 * FEATURES], F32)
+        def finish(m, proj, bank):
+            finish_columns(m, proj, bank * N_TILE, N_TILE)
+
+        bias_sb = keep.tile([P, 2 * FEATURES], BF16)
 
         def spread_biases():
-            for c in range(2 * BANKS):
-                cols = slice(c * N_TILE, (c + 1) * N_TILE)
-                spread = acc_pool.tile([P, N_TILE], F32, name="acc")
-                nc.tensor.matmul(
-                    out=spread[:], lhsT=ones[:], rhs=bias_rows[:, cols], start=True, stop=True
+            for proj in range(2):
+                spread = acc_pool.tile([P, FEATURES], BF16, name="acc")
+                for bank in range(BANKS):
+                    cols = slice(bank * N_TILE, (bank + 1) * N_TILE)
+                    nc.tensor.matmul(
+                        out=spread[:, cols],
+                        lhsT=ones[:],
+                        rhs=bias_rows[:, proj * FEATURES + bank * N_TILE : proj * FEATURES + (bank + 1) * N_TILE],
+                        start=True,
+                        stop=True,
+                    )
+                nc.scalar.copy(
+                    out=bias_sb[:, proj * FEATURES : (proj + 1) * FEATURES], in_=spread[:]
                 )
-                nc.scalar.copy(out=bias_sb[:, cols], in_=spread[:])
 
         with tc.manual_schedule():
             square(0)
             for r in range(NODE_TILES):
                 if r + 1 < NODE_TILES:
                     square(r + 1)
-                flip_nodes(r)
-                if r == 0:
+                flip_s(r)
+                flip_v(r)
+                empty_s(r)
+                empty_v(r)
+                if r == 1:
                     spread_biases()
+                if r == 4:
+                    regroup_weights(1, 0, 0, True)
                 if r < PASSES:
-                    fresh = [regroup_weights(0, r, bank, False) for bank in range(BANKS)]
                     for bank in range(BANKS):
-                        quantise_weights(0, r, bank, fresh[bank])
-                quantise_nodes(r)
-                if r >= LAG:
-                    g = r - LAG
-                    if g < PASSES:
-                        grouped = regroup_weights(1, g, 0, False)
-                    project(r - LAG, 0)
-                    if g < PASSES:
-                        quantise_weights(1, g, 0, grouped)
-            late = [regroup_weights(1, g, 1, True) for g in range(PASSES)]
+                        regroup_weights(0, r, bank)
+                    for bank in range(BANKS):
+                        quantise_weights(0, r, bank)
+                if r == 2:
+                    for m in range(2):
+                        for bank in range(BANKS):
+                            multiply_columns(m, 0, bank * N_TILE, N_TILE, range(S_PASSES))
+                if r <= 3:
+                    quantise_nodes(r)
+                if r == 3:
+                    for m in range(2):
+                        for bank in range(BANKS):
+                            multiply_columns(m, 0, bank * N_TILE, N_TILE, range(S_PASSES, PASSES))
+                    for m in range(2):
+                        for bank in range(BANKS):
+                            finish(m, 0, bank)
+                if r > 3:
+                    if r > 4:
+                        quantise_weights(1, r - 5, 0)
+                    if 4 < r < 7:
+                        regroup_weights(1, r - 4, 0)
+                    for bank in range(BANKS):
+                        multiply(r - 2, 0, bank)
+                        finish(r - 2, 0, bank)
+                    quantise_nodes(r)
             for g in range(PASSES):
-                project(NODE_TILES - LAG + g, 0)
-                quantise_weights(1, g, 1, late[g])
+                regroup_weights(1, g, 1, True)
+            for m in range(6, NODE_TILES):
+                for bank in range(BANKS):
+                    multiply(m, 0, bank)
+                    finish(m, 0, bank)
             for bank in range(BANKS):
-                cols = slice(bank * N_TILE, (bank + 1) * N_TILE)
                 for m in range(NODE_TILES):
-                    half = wide.tile([P, N_TILE], F32)
-                    project_bank(m, 1, bank, half[:])
-                    nc.sync.dma_start(out=out_rows[1][:, m, cols], in_=half[:])
+                    multiply(m, 1, bank)
+                    finish(m, 1, bank)
+                    if bank == 0 and m in (1, 3, 5):
+                        quantise_weights(1, m // 2, 1)

import concourse.mybir as mybir
from concourse.masks import make_identity

F32 = mybir.dt.float32
BF16 = mybir.dt.bfloat16
U32 = mybir.dt.uint32
U8 = mybir.dt.uint8
I32 = mybir.dt.int32
FP8X4 = mybir.dt.float8_e4m3fn_x4
ACT = mybir.ActivationFunctionType
ALU = mybir.AluOpType

P = 128
PACK = 4
K_PASS = P * PACK
NODES, NS, NV, XYZ = 1024, 1024, 512, 3
FEATURES = 1024
S_PASSES = NS // K_PASS
PASSES = (NS + NV) // K_PASS
NODE_TILES = NODES // P
PAIRS = NODE_TILES // 2
N_TILE = 512
BANKS = FEATURES // N_TILE
LAG = 3
NORM_FLOOR = 1e-4
SQRT_GUARD = 1e-30

FLOPS = 2 * NODES * (NS + NV) * 2 * FEATURES


def tile_multiattentivegvplayer_pa_kernel(tc, s, v, Wq, bq, Wk, bk, out_0, out_1):
    nc = tc.nc
    weights = (Wq, Wk)
    biases = (bq, bk)
    s_rows = s.rearrange("(p t) k -> p t k", t=NODE_TILES)
    v_rows = v.rearrange("(p t) j c -> p t (j c)", t=NODE_TILES)
    out_rows = (
        out_0.rearrange("(p t) h d -> p t (h d)", t=NODE_TILES),
        out_1.rearrange("(p t) h d -> p t (h d)", t=NODE_TILES),
    )

    with tc.tile_pool(name="keep", bufs=1) as keep, tc.tile_pool(
        name="stage", bufs=3
    ) as stage, tc.tile_pool(name="wide", bufs=4) as wide, tc.tile_pool(
        name="q_results", bufs=4
    ) as q_pool, tc.tile_pool(name="k_results", bufs=8) as k_pool, tc.psum_pool(name="flip", bufs=2) as flip, tc.psum_pool(
        name="acc", bufs=4
    ) as acc_pool:
        ident = keep.tile([P, P], F32)
        make_identity(nc, ident[:])
        ones = keep.tile([P, P], BF16)
        nc.vector.memset(ones[:], 1.0)
        filler = keep.tile([P, N_TILE], BF16)
        nc.vector.memset(filler[:].bitcast(I32), 0)
        one = keep.tile([P, 1], F32)
        nc.vector.memset(one[:], 1.0)

        bias_rows = keep.tile([P, 2 * FEATURES], BF16)
        nc.vector.memset(bias_rows[:].bitcast(I32), 0)
        for proj in range(2):
            nc.scalar.dma_start(
                out=bias_rows[0:1, proj * FEATURES : (proj + 1) * FEATURES],
                in_=biases[proj].unsqueeze(0),
            )
        root = keep.tile([P, 1], F32)
        nc.scalar.activation(out=root[:], in_=one[:], func=ACT.Sqrt)

        s_sb = {}
        v_sb = {}
        w_raw = {}

        def load_v(first, count):
            v_tiles = keep.tile([P, count, NV * XYZ], BF16, name="v_tiles%d" % first)
            nc.sync.dma_start(out=v_tiles[:], in_=v_rows[:, first : first + count, :])
            for i in range(count):
                v_sb[first + i] = v_tiles[:, i, :]

        def load_s(first, count):
            s_tiles = keep.tile([P, count, NS], BF16, name="s_tiles%d" % first)
            nc.sync.dma_start(out=s_tiles[:], in_=s_rows[:, first : first + count, :])
            for i in range(count):
                s_sb[first + i] = s_tiles[:, i, :]

        def load_columns(proj, g, bank):
            raw = keep.tile([P, PACK, N_TILE], BF16, name="w_raw%d_%d_%d" % (proj, g, bank))
            cols = slice(bank * N_TILE, (bank + 1) * N_TILE)
            rows = weights[proj][g * K_PASS : (g + 1) * K_PASS, cols]
            if g < S_PASSES:
                for u in range(2):
                    nc.sync.dma_start(
                        out=raw[:, 2 * u : 2 * u + 2, :],
                        in_=rows[u * 2 * P : (u + 1) * 2 * P, :].rearrange("(q e) c -> q e c", e=2),
                    )
            else:
                nc.sync.dma_start(out=raw[:], in_=rows.rearrange("(t q) c -> q t c", q=P))
            w_raw[proj, g, bank] = raw[:]

        def load_rows(proj, g):
            raw = keep.tile([P, PACK, FEATURES], BF16, name="w_raw%d_%d" % (proj, g))
            rows = weights[proj][g * K_PASS : (g + 1) * K_PASS, :]
            if g < S_PASSES:
                nc.sync.dma_start(
                    out=raw[:].rearrange("q (u e) c -> q u e c", u=2),
                    in_=rows.rearrange("(u q e) c -> q u e c", u=2, e=2),
                )
            else:
                nc.sync.dma_start(out=raw[:], in_=rows.rearrange("(t q) c -> q t c", q=P))
            for bank in range(BANKS):
                w_raw[proj, g, bank] = raw[:, :, bank * N_TILE : (bank + 1) * N_TILE]

        load_v(0, 2)
        load_rows(0, 0)
        load_s(0, 2)
        load_rows(0, 1)
        load_v(2, 2)
        load_s(2, 2)
        load_rows(0, 2)
        load_v(4, 2)
        load_s(4, 2)
        load_rows(1, 0)
        load_rows(1, 1)
        load_v(6, 2)
        load_s(6, 2)
        load_rows(1, 2)

        w_codes = keep.tile([P, PASSES, 2 * FEATURES], U32, align_bytes=64)
        w_scales = keep.tile([P, PASSES, 2 * FEATURES], U8, align_bytes=64)
        c_codes = keep.tile([P, NODE_TILES, PASSES * P], U32, align_bytes=64)
        c_scales = keep.tile([P, NODE_TILES, PASSES * P], U8, align_bytes=64)

        grouped_weights = {}

        def regroup_weights(proj, g, bank, on_scalar=False):
            grouped = wide.tile([P, N_TILE, PACK], BF16, align_bytes=64, name="w_grouped")
            dst = grouped[:].rearrange("p (c i) t -> p c t i", i=4)
            src = w_raw[proj, g, bank].rearrange("p t (c i) -> p c t i", i=4)
            if on_scalar:
                nc.scalar.copy(out=dst, in_=src)
            else:
                nc.vector.tensor_copy(out=dst, in_=src)
            grouped_weights[proj, g, bank] = grouped

        def quantise_weights(proj, g, bank):
            grouped = grouped_weights[proj, g, bank]
            first = proj * FEATURES + bank * N_TILE
            cols = slice(first, first + N_TILE)
            nc.vector.quantize_mx(
                out=w_codes[:, g, cols].bitcast(FP8X4),
                scales=w_scales[:, g, cols],
                in_=grouped[:].rearrange("p w t -> p (w t)"),
            )

        squares = {}
        grouped_s = {}
        roots = {}
        flipped = {}

        def square(m):
            sq = stage.tile([P, XYZ, NV], F32)
            nc.scalar.activation(
                out=sq[:], in_=v_sb[m].rearrange("p (j c) -> p c j", c=XYZ), func=ACT.Square
            )
            squares[m] = sq

        def flip_s(m):
            s_words = s_sb[m].bitcast(F32)
            s_flip = flip.tile([P, 2 * S_PASSES, P], F32, name="s_flip")
            for b in range(2 * S_PASSES):
                nc.tensor.transpose(s_flip[:, b, :], s_words[:, b * P : (b + 1) * P], ident[:])
            flipped[m, 0] = s_flip

        def flip_v(m, words=range(PACK)):
            if words[0] == 0:
                flipped[m, 1] = flip.tile([P, PACK, P], F32, name="n_flip")
            for t in words:
                for c in range(XYZ):
                    nc.tensor.matmul(
                        out=flipped[m, 1][:, t, :],
                        lhsT=squares[m][:, c, t * P : (t + 1) * P],
                        rhs=ident[:],
                        is_transpose=True,
                        start=(c == 0),
                        stop=(c == XYZ - 1),
                    )

        def keep_warm(count):
            spare = acc_pool.tile([P, N_TILE], F32, name="acc")
            for i in range(count):
                nc.tensor.matmul(
                    out=spare[:], lhsT=ones[:], rhs=filler[:], start=True, stop=True
                )

        def empty_s(m):
            s_grouped = stage.tile([P, S_PASSES, P, PACK], BF16, align_bytes=64)
            nc.scalar.copy(
                out=s_grouped[:].bitcast(F32),
                in_=flipped[m, 0][:].rearrange("p (g u) r -> p g r u", u=2),
            )
            grouped_s[m] = s_grouped

        def empty_v(m):
            n_root = stage.tile([P, P, PACK], BF16)
            nc.scalar.activation(
                out=n_root[:],
                in_=flipped[m, 1][:].rearrange("p t r -> p r t"),
                func=ACT.Sqrt,
                bias=SQRT_GUARD,
            )
            roots[m] = n_root

        def quantise_nodes(m):
            n_grouped = stage.tile([P, P, PACK], BF16, align_bytes=64)
            nc.vector.tensor_scalar_max(out=n_grouped[:], in0=roots[m][:], scalar1=NORM_FLOOR)
            nc.vector.quantize_mx(
                out=c_codes[:, m, 0 : S_PASSES * P].bitcast(FP8X4),
                scales=c_scales[:, m, 0 : S_PASSES * P],
                in_=grouped_s[m][:].rearrange("p g r t -> p (g r t)"),
            )
            nc.vector.quantize_mx(
                out=c_codes[:, m, S_PASSES * P : PASSES * P].bitcast(FP8X4),
                scales=c_scales[:, m, S_PASSES * P : PASSES * P],
                in_=n_grouped[:].rearrange("p r t -> p (r t)"),
            )

        sums = {}

        def multiply_columns(m, proj, first, width, passes=range(PASSES)):
            cols = slice(proj * FEATURES + first, proj * FEATURES + first + width)
            if passes[0] == 0:
                sums[m, proj, first] = acc_pool.tile([P, width], F32, name="acc")
            for g in passes:
                rows = slice(g * P, (g + 1) * P)
                nc.tensor.matmul_mx(
                    out=sums[m, proj, first][:],
                    lhsT=c_codes[:, m, rows].bitcast(FP8X4),
                    lhsT_scale=c_scales[:, m, rows],
                    rhs=w_codes[:, g, cols].bitcast(FP8X4),
                    rhs_scale=w_scales[:, g, cols],
                    start=(g == 0),
                    stop=(g == PASSES - 1),
                )

        q_results = {}

        def finish_columns(m, proj, first, width):
            if proj == 1:
                result = k_pool.tile([P, width], F32, name="k_result")[:]
            else:
                if first == 0:
                    q_results[m] = q_pool.tile([P, FEATURES], F32, name="q_result")
                result = q_results[m][:, first : first + width]
            nc.vector.tensor_tensor(
                out=result,
                in0=sums[m, proj, first][:],
                in1=bias_sb[:, proj * FEATURES + first : proj * FEATURES + first + width],
                op=ALU.add,
            )
            if proj == 1:
                nc.sync.dma_start(out=out_rows[1][:, m, first : first + width], in_=result)
            elif first + width == FEATURES:
                nc.sync.dma_start(out=out_rows[0][:, m, :], in_=q_results[m][:])

        def multiply(m, proj, bank):
            multiply_columns(m, proj, bank * N_TILE, N_TILE)

        def finish(m, proj, bank):
            finish_columns(m, proj, bank * N_TILE, N_TILE)

        bias_sb = keep.tile([P, 2 * FEATURES], BF16)

        def spread_biases():
            for proj in range(2):
                spread = acc_pool.tile([P, FEATURES], BF16, name="acc")
                for bank in range(BANKS):
                    cols = slice(bank * N_TILE, (bank + 1) * N_TILE)
                    nc.tensor.matmul(
                        out=spread[:, cols],
                        lhsT=ones[:],
                        rhs=bias_rows[:, proj * FEATURES + bank * N_TILE : proj * FEATURES + (bank + 1) * N_TILE],
                        start=True,
                        stop=True,
                    )
                nc.scalar.copy(
                    out=bias_sb[:, proj * FEATURES : (proj + 1) * FEATURES], in_=spread[:]
                )

        with tc.manual_schedule():
            square(0)
            for r in range(NODE_TILES):
                if r + 1 < NODE_TILES:
                    square(r + 1)
                flip_s(r)
                flip_v(r)
                empty_s(r)
                empty_v(r)
                if r == 1:
                    spread_biases()
                if r == 4:
                    regroup_weights(1, 0, 0, True)
                if r < PASSES:
                    for bank in range(BANKS):
                        regroup_weights(0, r, bank)
                    for bank in range(BANKS):
                        quantise_weights(0, r, bank)
                if r == 2:
                    for m in range(2):
                        for bank in range(BANKS):
                            multiply_columns(m, 0, bank * N_TILE, N_TILE, range(S_PASSES))
                if r <= 3:
                    quantise_nodes(r)
                if r == 3:
                    for m in range(2):
                        for bank in range(BANKS):
                            multiply_columns(m, 0, bank * N_TILE, N_TILE, range(S_PASSES, PASSES))
                    for m in range(2):
                        for bank in range(BANKS):
                            finish(m, 0, bank)
                if r > 3:
                    if r > 4:
                        quantise_weights(1, r - 5, 0)
                    if 4 < r < 7:
                        regroup_weights(1, r - 4, 0)
                    for bank in range(BANKS):
                        multiply(r - 2, 0, bank)
                        finish(r - 2, 0, bank)
                    quantise_nodes(r)
            for g in range(PASSES):
                regroup_weights(1, g, 1, True)
            for m in range(6, NODE_TILES):
                for bank in range(BANKS):
                    multiply(m, 0, bank)
                    finish(m, 0, bank)
            for bank in range(BANKS):
                for m in range(NODE_TILES):
                    multiply(m, 1, bank)
                    finish(m, 1, bank)
                    if bank == 0 and m in (1, 3, 5):
                        quantise_weights(1, m // 2, 1)
